import numpy as np
import ml_dtypes


def mxq(x, axis, fmt="e4m3"):
    dtype, down = {"e4m3": (ml_dtypes.float8_e4m3fn, 7), "e5m2": (ml_dtypes.float8_e5m2, 14)}[fmt]
    v = np.moveaxis(np.asarray(x, np.float32).astype(ml_dtypes.bfloat16).astype(np.float64), axis, -1)
    blocks = v.reshape(v.shape[:-1] + (-1, 32))
    amax = np.abs(blocks).max(-1, keepdims=True)
    byte = np.maximum(np.where(amax > 0, np.frexp(amax)[1] - 1 + 127, 0) - down, 1)
    scale = np.exp2(byte - 127.0)
    codes = (blocks / scale).astype(np.float32).astype(dtype).astype(np.float64)
    return np.moveaxis((codes * scale).reshape(v.shape), -1, axis)


WIDE = False


def mx_kscale(k):
    if not WIDE:
        return np.ones(k)
    levels = np.array([10, -10, 5, -5, 0])
    a = np.random.permutation(np.resize(levels, k // 512 * 4)).reshape(k // 512, 4)
    idx = np.arange(k)
    return np.exp2(a[idx // 512, idx % 128 // 32])


BF16 = ml_dtypes.bfloat16


def bf(x):
    return np.asarray(x, np.float32).astype(BF16)


def f64(x):
    return np.asarray(x).astype(np.float64)


B, T, D, H, HD = 2, 512, 1024, 8, 128
E = H * HD


def rope(u):
    inv_freq = 1.0 / (10000.0 ** (f64(np.arange(0, HD, 2)) / HD))
    pe = f64(np.arange(T))[:, None] * inv_freq[None, :]
    pe = np.repeat(pe, 2, axis=-1)
    u1 = u[..., 0::2]
    u2 = u[..., 1::2]
    rot = np.stack((-u2, u1), axis=-1).reshape(u.shape)
    return u * np.cos(pe) + rot * np.sin(pe)


def split_heads(u):
    return u.reshape(B, T, H, HD).transpose(0, 2, 1, 3)


def setup_inputs():
    s = mx_kscale(D)
    return {"x": bf(np.random.standard_normal((B, T, D)) * s),
            "w_qkv": bf(np.random.standard_normal((D, 3 * E)) / np.sqrt(D) / s[:, None])}


def reference(x, w_qkv):
    qkv = mxq(f64(x), 2, "e4m3") @ mxq(f64(w_qkv), 0, "e4m3")
    q, k, v = np.split(qkv, 3, axis=2)
    q, k, v = split_heads(q), split_heads(k), split_heads(v)
    return rope(q), rope(k), v

@@ -1,0 +1,249 @@
+import math
+from contextlib import ExitStack
+
+import concourse.mybir as mybir
+from concourse.masks import make_identity
+
+F32 = mybir.dt.float32
+BF16 = mybir.dt.bfloat16
+I32 = mybir.dt.int32
+U32 = mybir.dt.uint32
+U8 = mybir.dt.uint8
+FP8X4 = mybir.dt.float8_e4m3fn_x4
+ALU = mybir.AluOpType
+ACT = mybir.ActivationFunctionType
+
+B, T, D, H, HD = 2, 512, 1024, 8, 128
+E = H * HD
+FLOPS = 2 * B * T * D * 3 * E
+
+P = 128
+PACK = 4
+K_PASS = P * PACK
+PASSES = D // K_PASS
+WORDS = PACK // 2
+TOKEN_TILES = T // P
+CHUNK = 512
+CHUNK_HEADS = CHUNK // HD
+ROPE_CHUNKS = 2 * E // CHUNK
+PLAIN_CHUNKS = E // CHUNK
+PAIRS = HD // 2
+DOUBLINGS = 6
+assert 2**DOUBLINGS == PAIRS
+RUN = 4
+ADD_TILES = 2
+
+TURN = 2.0 * math.pi
+FREQ_RATIO = 10000.0 ** (-2.0 / HD)
+ROUND_MAGIC = 1.5 * 2.0**23
+
+
+def wrap_turns(nc, pool, out, turns, name):
+    nearest = pool.tile([P, TOKEN_TILES, PAIRS], F32, name=name)
+    nc.vector.tensor_scalar(
+        out=nearest[:], in0=turns, scalar1=ROUND_MAGIC, scalar2=ROUND_MAGIC, op0=ALU.add, op1=ALU.subtract
+    )
+    nc.vector.tensor_tensor(out=out, in0=turns, in1=nearest[:], op=ALU.subtract)
+
+
+def build_rope_tables(nc, pool):
+    shape = [P, TOKEN_TILES, PAIRS]
+    token_int = pool.tile([P, TOKEN_TILES], I32)
+    nc.gpsimd.iota(token_int[:], pattern=[[1, TOKEN_TILES]], base=0, channel_multiplier=TOKEN_TILES)
+    token = pool.tile([P, TOKEN_TILES], F32)
+    nc.vector.tensor_copy(out=token[:], in_=token_int[:])
+
+    one = pool.tile([P, 1], F32)
+    nc.vector.memset(one[:], 1.0)
+    turns_per_token = pool.tile([P, PAIRS], F32)
+    nc.vector.tensor_scalar_mul(out=turns_per_token[:, 0:1], in0=one[:], scalar1=1.0 / TURN)
+    for doubling in range(DOUBLINGS):
+        width = 2**doubling
+        nc.vector.tensor_scalar_mul(
+            out=turns_per_token[:, width : 2 * width], in0=turns_per_token[:, 0:width], scalar1=FREQ_RATIO**width
+        )
+
+    turns = pool.tile(shape, F32)
+    nc.vector.tensor_tensor(
+        out=turns[:],
+        in0=token[:].unsqueeze(2).to_broadcast(shape),
+        in1=turns_per_token[:].unsqueeze(1).to_broadcast(shape),
+        op=ALU.mult,
+    )
+    sin_turns = pool.tile(shape, F32)
+    wrap_turns(nc, pool, sin_turns[:], turns[:], "nearest_sin")
+    quarter_on = pool.tile(shape, F32)
+    nc.vector.tensor_scalar_add(out=quarter_on[:], in0=sin_turns[:], scalar1=0.25)
+    cos_turns = pool.tile(shape, F32)
+    wrap_turns(nc, pool, cos_turns[:], quarter_on[:], "nearest_cos")
+
+    cos_both = pool.tile([P, TOKEN_TILES, HD], F32)
+    nc.scalar.activation(
+        out=cos_both[:].rearrange("p j (i e) -> p j i e", e=2),
+        in_=cos_turns[:].unsqueeze(3).to_broadcast(shape + [2]),
+        func=ACT.Sin,
+        scale=TURN,
+    )
+    sin_signed = pool.tile([P, TOKEN_TILES, 2, PAIRS], F32)
+    nc.scalar.activation(out=sin_signed[:, :, 0, :], in_=sin_turns[:], func=ACT.Sin, scale=-TURN)
+    nc.scalar.activation(out=sin_signed[:, :, 1, :], in_=sin_turns[:], func=ACT.Sin, scale=TURN)
+    return cos_both, sin_signed
+
+
+def tile_selfattention_pa_kernel(tc, x, w_qkv, out_0, out_1, out_2):
+    nc = tc.nc
+    with ExitStack() as ctx:
+        const = ctx.enter_context(tc.tile_pool(name="const", bufs=1))
+        keep = ctx.enter_context(tc.tile_pool(name="keep", bufs=1))
+        grouped_pool = ctx.enter_context(tc.tile_pool(name="grouped", bufs=3))
+        work = ctx.enter_context(tc.tile_pool(name="work", bufs=3))
+        results = ctx.enter_context(tc.tile_pool(name="results", bufs=4))
+        psum = ctx.enter_context(tc.psum_pool(name="psum", bufs=8))
+
+        units = []
+        chunk_order = []
+        for r in range(ROPE_CHUNKS):
+            plain = ROPE_CHUNKS + r // B
+            chunk_order.append(r)
+            if plain not in chunk_order:
+                chunk_order.append(plain)
+            units.extend([(r, 0), (plain, r % B), (r, 1)])
+
+        x_raw = keep.tile([P, B, TOKEN_TILES, D], BF16)
+        x_rows = x.rearrange("b (p j) k -> b p j k", j=TOKEN_TILES)
+        w_rows = w_qkv.rearrange("(g p r) c -> g p r c", g=PASSES, r=PACK)
+        w_raw = {}
+
+        for n in chunk_order:
+            w_raw[n] = keep.tile([P, PASSES, PACK, CHUNK], BF16, name="w_raw%d" % n)
+
+        def load_w(n, g):
+            nc.sync.dma_start(out=w_raw[n][:, g], in_=w_rows[g, :, :, n * CHUNK : (n + 1) * CHUNK])
+
+        def load_x(b, j):
+            nc.sync.dma_start(out=x_raw[:, b, j], in_=x_rows[b, :, j])
+
+        load_w(chunk_order[0], 0)
+        load_x(0, 0)
+        load_w(chunk_order[0], 1)
+        for j in range(1, TOKEN_TILES):
+            load_x(0, j)
+        for g in range(PASSES):
+            load_w(chunk_order[1], g)
+        for j in range(TOKEN_TILES):
+            load_x(1, j)
+        for n in chunk_order[2:]:
+            for g in range(PASSES):
+                load_w(n, g)
+
+        identity = const.tile([P, P], F32)
+        make_identity(nc, identity[:])
+        cos_both, sin_signed = build_rope_tables(nc, const)
+
+        w_codes = {}
+        w_scales = {}
+
+        def quantise_chunk(n, copy):
+            grouped = grouped_pool.tile([P, PASSES, CHUNK, PACK], BF16, name="w_grouped", align_bytes=64)
+            w_codes[n] = keep.tile([P, PASSES, CHUNK], U32, name="w_codes%d" % n, align_bytes=64)
+            w_scales[n] = keep.tile([P, PASSES, CHUNK], U8, name="w_scales%d" % n, align_bytes=64)
+            for g in range(PASSES):
+                copy(
+                    out=grouped[:, g].rearrange("p (c i) r -> p c r i", i=RUN),
+                    in_=w_raw[n][:, g].rearrange("p r (c i) -> p c r i", i=RUN),
+                )
+            for g in range(PASSES):
+                nc.vector.quantize_mx(
+                    out=w_codes[n][:, g].bitcast(FP8X4),
+                    scales=w_scales[n][:, g],
+                    in_=grouped[:, g].rearrange("p c r -> p (c r)"),
+                )
+
+        x_grouped = keep.tile([P, B, TOKEN_TILES, PASSES, P, PACK], BF16, align_bytes=64)
+        x_codes = keep.tile([P, B, TOKEN_TILES, PASSES, P], U32, align_bytes=64)
+        x_scales = keep.tile([P, B, TOKEN_TILES, PASSES, P], U8, align_bytes=64)
+        x_words = x_raw[:].bitcast(F32).rearrange("p b j (g q u) -> p b j g u q", g=PASSES, u=WORDS)
+
+        def quantise_batch(b):
+            for j in range(TOKEN_TILES):
+                flipped = psum.tile([P, PASSES, WORDS, P], F32, name="flipped", tag="bank")
+                for g in range(PASSES):
+                    for u in range(WORDS):
+                        nc.tensor.transpose(flipped[:, g, u, :], x_words[:, b, j, g, u, :], identity[:])
+                nc.scalar.copy(
+                    out=x_grouped[:, b, j].bitcast(F32), in_=flipped[:].rearrange("p g u t -> p g t u")
+                )
+            for j in range(TOKEN_TILES):
+                nc.vector.quantize_mx(
+                    out=x_codes[:, b, j].rearrange("p g t -> p (g t)").bitcast(FP8X4),
+                    scales=x_scales[:, b, j].rearrange("p g t -> p (g t)"),
+                    in_=x_grouped[:, b, j].rearrange("p g t r -> p (g t r)"),
+                )
+
+        def project(n, b, j):
+            bank = psum.tile([P, CHUNK], F32, name="bank", tag="bank")
+            for g in range(PASSES):
+                nc.tensor.matmul_mx(
+                    out=bank[:],
+                    lhsT=x_codes[:, b, j, g, :].bitcast(FP8X4),
+                    lhsT_scale=x_scales[:, b, j, g, :],
+                    rhs=w_codes[n][:, g, :].bitcast(FP8X4),
+                    rhs_scale=w_scales[n][:, g, :],
+                    start=(g == 0),
+                    stop=(g == PASSES - 1),
+                )
+            return bank
+
+        def rotate(n, b, first_j, rotated):
+            by_cos = work.tile([P, CHUNK_HEADS, ADD_TILES, HD], F32, name="by_cos")
+            by_sin = work.tile([P, 2, CHUNK_HEADS, ADD_TILES, PAIRS], F32, name="by_sin")
+            for a in range(ADD_TILES):
+                j = first_j + a
+                bank = project(n, b, j)
+                nc.vector.tensor_tensor(
+                    out=by_cos[:, :, a, :],
+                    in0=bank[:].rearrange("p (h d) -> p h d", h=CHUNK_HEADS),
+                    in1=cos_both[:, j, :].unsqueeze(1).to_broadcast([P, CHUNK_HEADS, HD]),
+                    op=ALU.mult,
+                )
+                members = bank[:].rearrange("p (h i e) -> p h i e", h=CHUNK_HEADS, e=2)
+                for e in range(2):
+                    nc.vector.tensor_tensor(
+                        out=by_sin[:, e, :, a, :],
+                        in0=members[:, :, :, 1 - e],
+                        in1=sin_signed[:, j, e, :].unsqueeze(1).to_broadcast([P, CHUNK_HEADS, PAIRS]),
+                        op=ALU.mult,
+                    )
+            nc.gpsimd.tensor_tensor(
+                out=rotated.rearrange("p h a (i e) -> p h (a i) e", e=2),
+                in0=by_cos[:].rearrange("p h a (i e) -> p h (a i) e", e=2),
+                in1=by_sin[:].rearrange("p e h a i -> p h (a i) e"),
+                op=ALU.add,
+            )
+
+        def run_unit(n, b):
+            out = (out_0, out_1, out_2)[n * CHUNK // E]
+            first_head = n * CHUNK % E // HD
+            result = results.tile([P, CHUNK_HEADS, TOKEN_TILES, HD], F32, name="result")
+            if n < ROPE_CHUNKS:
+                for first_j in range(0, TOKEN_TILES, ADD_TILES):
+                    rotate(n, b, first_j, result[:, :, first_j : first_j + ADD_TILES, :])
+            else:
+                for j in range(TOKEN_TILES):
+                    bank = project(n, b, j)
+                    nc.scalar.copy(out=result[:, :, j, :], in_=bank[:].rearrange("p (h d) -> p h d", h=CHUNK_HEADS))
+            nc.sync.dma_start(
+                out=out[b, first_head : first_head + CHUNK_HEADS].rearrange("h (p j) d -> p h (j d)", j=TOKEN_TILES),
+                in_=result[:].rearrange("p h j d -> p h (j d)"),
+            )
+
+        quantise_chunk(chunk_order[0], nc.vector.tensor_copy)
+        quantise_batch(0)
+        ready = 1
+        for step, (n, b) in enumerate(units):
+            if ready < len(chunk_order):
+                quantise_chunk(chunk_order[ready], nc.scalar.copy)
+                ready += 1
+            run_unit(n, b)
+            if step == 0:
+                quantise_batch(1)

@@ -84,9 +84,9 @@ def build_rope_tables(nc, pool):
         func=ACT.Sin,
         scale=TURN,
     )
-    sin_signed = pool.tile([P, TOKEN_TILES, 2, PAIRS], F32)
-    nc.scalar.activation(out=sin_signed[:, :, 0, :], in_=sin_turns[:], func=ACT.Sin, scale=-TURN)
-    nc.scalar.activation(out=sin_signed[:, :, 1, :], in_=sin_turns[:], func=ACT.Sin, scale=TURN)
+    sin_signed = pool.tile([P, TOKEN_TILES, PAIRS, 2], F32)
+    nc.scalar.activation(out=sin_signed[:, :, :, 0], in_=sin_turns[:], func=ACT.Sin, scale=-TURN)
+    nc.scalar.activation(out=sin_signed[:, :, :, 1], in_=sin_turns[:], func=ACT.Sin, scale=TURN)
     return cos_both, sin_signed
 
 
@@ -196,7 +196,7 @@ def tile_selfattention_pa_kernel(tc, x, w_qkv, out_0, out_1, out_2):
 
         def rotate(n, b, first_j, rotated):
             by_cos = work.tile([P, CHUNK_HEADS, ADD_TILES, HD], F32, name="by_cos")
-            by_sin = work.tile([P, 2, CHUNK_HEADS, ADD_TILES, PAIRS], F32, name="by_sin")
+            by_sin = work.tile([P, CHUNK_HEADS, ADD_TILES, HD], F32, name="by_sin")
             for a in range(ADD_TILES):
                 j = first_j + a
                 bank = project(n, b, j)
@@ -207,17 +207,16 @@ def tile_selfattention_pa_kernel(tc, x, w_qkv, out_0, out_1, out_2):
                     op=ALU.mult,
                 )
                 members = bank[:].rearrange("p (h i e) -> p h i e", h=CHUNK_HEADS, e=2)
-                for e in range(2):
-                    nc.vector.tensor_tensor(
-                        out=by_sin[:, e, :, a, :],
-                        in0=members[:, :, :, 1 - e],
-                        in1=sin_signed[:, j, e, :].unsqueeze(1).to_broadcast([P, CHUNK_HEADS, PAIRS]),
-                        op=ALU.mult,
-                    )
+                nc.vector.tensor_tensor(
+                    out=by_sin[:, :, a, :].rearrange("p h (i e) -> p h i e", e=2),
+                    in0=members[:, :, :, ::-1],
+                    in1=sin_signed[:, j].unsqueeze(1).to_broadcast([P, CHUNK_HEADS, PAIRS, 2]),
+                    op=ALU.mult,
+                )
             nc.gpsimd.tensor_tensor(
-                out=rotated.rearrange("p h a (i e) -> p h (a i) e", e=2),
-                in0=by_cos[:].rearrange("p h a (i e) -> p h (a i) e", e=2),
-                in1=by_sin[:].rearrange("p e h a i -> p h (a i) e"),
+                out=rotated.rearrange("p h a d -> p h (a d)"),
+                in0=by_cos[:].rearrange("p h a d -> p h (a d)"),
+                in1=by_sin[:].rearrange("p h a d -> p h (a d)"),
                 op=ALU.add,
             )
 

@@ -32,6 +32,8 @@ DOUBLINGS = 6
 assert 2**DOUBLINGS == PAIRS
 RUN = 4
 ADD_TILES = 2
+WORK_BUFS = 4
+VECTOR_ADDS = (15,)
 
 TURN = 2.0 * math.pi
 FREQ_RATIO = 10000.0 ** (-2.0 / HD)
@@ -96,92 +98,92 @@ def tile_selfattention_pa_kernel(tc, x, w_qkv, out_0, out_1, out_2):
         const = ctx.enter_context(tc.tile_pool(name="const", bufs=1))
         keep = ctx.enter_context(tc.tile_pool(name="keep", bufs=1))
         grouped_pool = ctx.enter_context(tc.tile_pool(name="grouped", bufs=3))
-        work = ctx.enter_context(tc.tile_pool(name="work", bufs=3))
-        results = ctx.enter_context(tc.tile_pool(name="results", bufs=4))
-        psum = ctx.enter_context(tc.psum_pool(name="psum", bufs=8))
+        work = ctx.enter_context(tc.tile_pool(name="work", bufs=WORK_BUFS))
+        results = ctx.enter_context(tc.tile_pool(name="results", bufs=3))
+        psum = ctx.enter_context(tc.psum_pool(name="psum", bufs=4))
+        ctx.enter_context(tc.manual_schedule())
 
-        units = []
-        chunk_order = []
-        for r in range(ROPE_CHUNKS):
-            plain = ROPE_CHUNKS + r // B
-            chunk_order.append(r)
-            if plain not in chunk_order:
-                chunk_order.append(plain)
-            units.extend([(r, 0), (plain, r % B), (r, 1)])
+        warm = const.tile([P, 1], F32)
+        nc.vector.memset(warm[:], 0.0)
+        nc.scalar.activation(out=warm[:], in_=warm[:], func=ACT.Sin)
 
         x_raw = keep.tile([P, B, TOKEN_TILES, D], BF16)
         x_rows = x.rearrange("b (p j) k -> b p j k", j=TOKEN_TILES)
         w_rows = w_qkv.rearrange("(g p r) c -> g p r c", g=PASSES, r=PACK)
         w_raw = {}
 
-        for n in chunk_order:
-            w_raw[n] = keep.tile([P, PASSES, PACK, CHUNK], BF16, name="w_raw%d" % n)
+        def load_w(first_chunk, chunks, g):
+            piece = keep.tile([P, PACK, chunks * CHUNK], BF16, name="w_raw%d_%d" % (first_chunk, g))
+            nc.sync.dma_start(out=piece[:], in_=w_rows[g, :, :, first_chunk * CHUNK : (first_chunk + chunks) * CHUNK])
+            for c in range(chunks):
+                w_raw[(first_chunk + c, g)] = piece[:, :, c * CHUNK : (c + 1) * CHUNK]
 
-        def load_w(n, g):
-            nc.sync.dma_start(out=w_raw[n][:, g], in_=w_rows[g, :, :, n * CHUNK : (n + 1) * CHUNK])
+        def load_x(b, j, tiles):
+            nc.sync.dma_start(out=x_raw[:, b, j : j + tiles], in_=x_rows[b, :, j : j + tiles])
 
-        def load_x(b, j):
-            nc.sync.dma_start(out=x_raw[:, b, j], in_=x_rows[b, :, j])
-
-        load_w(chunk_order[0], 0)
-        load_x(0, 0)
-        load_w(chunk_order[0], 1)
-        for j in range(1, TOKEN_TILES):
-            load_x(0, j)
-        for g in range(PASSES):
-            load_w(chunk_order[1], g)
-        for j in range(TOKEN_TILES):
-            load_x(1, j)
-        for n in chunk_order[2:]:
-            for g in range(PASSES):
-                load_w(n, g)
+        load_x(0, 0, 1)
+        load_w(0, 1, 0)
+        load_w(0, 1, 1)
+        load_x(0, 1, 1)
+        load_x(0, 2, 2)
+        load_x(1, 0, 2)
+        load_w(1, 1, 0)
+        load_x(1, 2, 2)
+        load_w(1, 1, 1)
+        load_w(4, 2, 0)
+        load_w(4, 2, 1)
+        load_w(2, 2, 0)
+        load_w(2, 2, 1)
 
         identity = const.tile([P, P], F32)
         make_identity(nc, identity[:])
         cos_both, sin_signed = build_rope_tables(nc, const)
 
+        w_grouped = {}
         w_codes = {}
         w_scales = {}
 
-        def quantise_chunk(n, copy):
-            grouped = grouped_pool.tile([P, PASSES, CHUNK, PACK], BF16, name="w_grouped", align_bytes=64)
-            w_codes[n] = keep.tile([P, PASSES, CHUNK], U32, name="w_codes%d" % n, align_bytes=64)
-            w_scales[n] = keep.tile([P, PASSES, CHUNK], U8, name="w_scales%d" % n, align_bytes=64)
-            for g in range(PASSES):
-                copy(
-                    out=grouped[:, g].rearrange("p (c i) r -> p c r i", i=RUN),
-                    in_=w_raw[n][:, g].rearrange("p r (c i) -> p c r i", i=RUN),
-                )
-            for g in range(PASSES):
-                nc.vector.quantize_mx(
-                    out=w_codes[n][:, g].bitcast(FP8X4),
-                    scales=w_scales[n][:, g],
-                    in_=grouped[:, g].rearrange("p c r -> p (c r)"),
-                )
+        def regroup(n, g, copy):
+            if n not in w_grouped:
+                w_grouped[n] = grouped_pool.tile([P, PASSES, CHUNK, PACK], BF16, name="w_grouped", align_bytes=64)
+            copy(
+                out=w_grouped[n][:, g].rearrange("p (c i) r -> p c r i", i=RUN),
+                in_=w_raw[(n, g)].rearrange("p r (c i) -> p c r i", i=RUN),
+            )
+
+        def quantise_w(n, first_g, passes):
+            if n not in w_codes:
+                w_codes[n] = keep.tile([P, PASSES, CHUNK], U32, name="w_codes%d" % n, align_bytes=64)
+                w_scales[n] = keep.tile([P, PASSES, CHUNK], U8, name="w_scales%d" % n, align_bytes=64)
+            gs = slice(first_g, first_g + passes)
+            nc.vector.quantize_mx(
+                out=w_codes[n][:, gs].rearrange("p g c -> p (g c)").bitcast(FP8X4),
+                scales=w_scales[n][:, gs].rearrange("p g c -> p (g c)"),
+                in_=w_grouped[n][:, gs].rearrange("p g c r -> p (g c r)"),
+            )
 
         x_grouped = keep.tile([P, B, TOKEN_TILES, PASSES, P, PACK], BF16, align_bytes=64)
         x_codes = keep.tile([P, B, TOKEN_TILES, PASSES, P], U32, align_bytes=64)
         x_scales = keep.tile([P, B, TOKEN_TILES, PASSES, P], U8, align_bytes=64)
         x_words = x_raw[:].bitcast(F32).rearrange("p b j (g q u) -> p b j g u q", g=PASSES, u=WORDS)
 
-        def quantise_batch(b):
-            for j in range(TOKEN_TILES):
-                flipped = psum.tile([P, PASSES, WORDS, P], F32, name="flipped", tag="bank")
-                for g in range(PASSES):
-                    for u in range(WORDS):
-                        nc.tensor.transpose(flipped[:, g, u, :], x_words[:, b, j, g, u, :], identity[:])
-                nc.scalar.copy(
-                    out=x_grouped[:, b, j].bitcast(F32), in_=flipped[:].rearrange("p g u t -> p g t u")
-                )
-            for j in range(TOKEN_TILES):
-                nc.vector.quantize_mx(
-                    out=x_codes[:, b, j].rearrange("p g t -> p (g t)").bitcast(FP8X4),
-                    scales=x_scales[:, b, j].rearrange("p g t -> p (g t)"),
-                    in_=x_grouped[:, b, j].rearrange("p g t r -> p (g t r)"),
-                )
+        def flip(b, j):
+            flipped = psum.tile([P, PASSES, WORDS, P], F32, name="flipped", tag="plain")
+            for g in range(PASSES):
+                for u in range(WORDS):
+                    nc.tensor.transpose(flipped[:, g, u, :], x_words[:, b, j, g, u, :], identity[:])
+            nc.scalar.copy(out=x_grouped[:, b, j].bitcast(F32), in_=flipped[:].rearrange("p g u t -> p g t u"))
 
-        def project(n, b, j):
-            bank = psum.tile([P, CHUNK], F32, name="bank", tag="bank")
+        def quantise_x(b, j, tiles):
+            js = slice(j, j + tiles)
+            nc.vector.quantize_mx(
+                out=x_codes[:, b, js].rearrange("p j g t -> p (j g t)").bitcast(FP8X4),
+                scales=x_scales[:, b, js].rearrange("p j g t -> p (j g t)"),
+                in_=x_grouped[:, b, js].rearrange("p j g t r -> p (j g t r)"),
+            )
+
+        def project(n, b, j, tag):
+            bank = psum.tile([P, CHUNK], F32, name="bank_" + tag, tag=tag)
             for g in range(PASSES):
                 nc.tensor.matmul_mx(
                     out=bank[:],
@@ -194,55 +196,115 @@ def tile_selfattention_pa_kernel(tc, x, w_qkv, out_0, out_1, out_2):
                 )
             return bank
 
-        def rotate(n, b, first_j, rotated):
+        def destination(n, b):
+            out = (out_0, out_1, out_2)[n * CHUNK // E]
+            first_head = n * CHUNK % E // HD
+            return out[b, first_head : first_head + CHUNK_HEADS].rearrange("h (p j) d -> p h j d", j=TOKEN_TILES)
+
+        groups = [(n, b, j) for n in range(ROPE_CHUNKS) for b in range(B) for j in range(0, TOKEN_TILES, ADD_TILES)]
+        banks = {}
+        rope_result = {}
+
+        def project_group(i):
+            n, b, first_j = groups[i]
+            banks[i] = [project(n, b, first_j + a, "rope") for a in range(ADD_TILES)]
+
+        def rotate_group(i):
+            n, b, first_j = groups[i]
+            last_unit = i >= len(groups) - TOKEN_TILES // ADD_TILES
+            if last_unit:
+                half = results.tile([P, CHUNK_HEADS, ADD_TILES, HD], F32, name="rotated")
+                rotated = half[:]
+            else:
+                if first_j == 0:
+                    rope_result[(n, b)] = results.tile([P, CHUNK_HEADS, TOKEN_TILES, HD], F32, name="rotated")
+                rotated = rope_result[(n, b)][:, :, first_j : first_j + ADD_TILES, :]
             by_cos = work.tile([P, CHUNK_HEADS, ADD_TILES, HD], F32, name="by_cos")
             by_sin = work.tile([P, CHUNK_HEADS, ADD_TILES, HD], F32, name="by_sin")
             for a in range(ADD_TILES):
                 j = first_j + a
-                bank = project(n, b, j)
+                bank = banks[i][a]
                 nc.vector.tensor_tensor(
                     out=by_cos[:, :, a, :],
                     in0=bank[:].rearrange("p (h d) -> p h d", h=CHUNK_HEADS),
                     in1=cos_both[:, j, :].unsqueeze(1).to_broadcast([P, CHUNK_HEADS, HD]),
                     op=ALU.mult,
                 )
-                members = bank[:].rearrange("p (h i e) -> p h i e", h=CHUNK_HEADS, e=2)
                 nc.vector.tensor_tensor(
                     out=by_sin[:, :, a, :].rearrange("p h (i e) -> p h i e", e=2),
-                    in0=members[:, :, :, ::-1],
+                    in0=bank[:].rearrange("p (h i e) -> p h i e", h=CHUNK_HEADS, e=2)[:, :, :, ::-1],
                     in1=sin_signed[:, j].unsqueeze(1).to_broadcast([P, CHUNK_HEADS, PAIRS, 2]),
                     op=ALU.mult,
                 )
-            nc.gpsimd.tensor_tensor(
+            adder = nc.vector if i in VECTOR_ADDS else nc.gpsimd
+            adder.tensor_tensor(
                 out=rotated.rearrange("p h a d -> p h (a d)"),
                 in0=by_cos[:].rearrange("p h a d -> p h (a d)"),
                 in1=by_sin[:].rearrange("p h a d -> p h (a d)"),
                 op=ALU.add,
             )
+            if last_unit:
+                nc.sync.dma_start(out=destination(n, b)[:, :, first_j : first_j + ADD_TILES, :], in_=rotated)
+            elif first_j + ADD_TILES == TOKEN_TILES:
+                nc.sync.dma_start(out=destination(n, b), in_=rope_result[(n, b)][:])
 
-        def run_unit(n, b):
-            out = (out_0, out_1, out_2)[n * CHUNK // E]
-            first_head = n * CHUNK % E // HD
-            result = results.tile([P, CHUNK_HEADS, TOKEN_TILES, HD], F32, name="result")
-            if n < ROPE_CHUNKS:
-                for first_j in range(0, TOKEN_TILES, ADD_TILES):
-                    rotate(n, b, first_j, result[:, :, first_j : first_j + ADD_TILES, :])
-            else:
-                for j in range(TOKEN_TILES):
-                    bank = project(n, b, j)
-                    nc.scalar.copy(out=result[:, :, j, :], in_=bank[:].rearrange("p (h d) -> p h d", h=CHUNK_HEADS))
-            nc.sync.dma_start(
-                out=out[b, first_head : first_head + CHUNK_HEADS].rearrange("h (p j) d -> p h (j d)", j=TOKEN_TILES),
-                in_=result[:].rearrange("p h j d -> p h (j d)"),
-            )
+        plain = [(n, b, j) for n in range(ROPE_CHUNKS, ROPE_CHUNKS + PLAIN_CHUNKS) for b in range(B) for j in range(TOKEN_TILES)]
+        plain_result = {}
 
-        quantise_chunk(chunk_order[0], nc.vector.tensor_copy)
-        quantise_batch(0)
-        ready = 1
-        for step, (n, b) in enumerate(units):
-            if ready < len(chunk_order):
-                quantise_chunk(chunk_order[ready], nc.scalar.copy)
-                ready += 1
-            run_unit(n, b)
-            if step == 0:
-                quantise_batch(1)
+        def plain_bank(k):
+            n, b, j = plain[k]
+            if j == 0:
+                plain_result[(n, b)] = results.tile([P, CHUNK_HEADS, TOKEN_TILES, HD], F32, name="copied")
+            bank = project(n, b, j, "plain")
+            nc.scalar.copy(out=plain_result[(n, b)][:, :, j, :], in_=bank[:].rearrange("p (h d) -> p h d", h=CHUNK_HEADS))
+            if j == TOKEN_TILES - 1:
+                nc.scalar.dma_start(out=destination(n, b), in_=plain_result[(n, b)][:])
+
+        flip(0, 0)
+        regroup(0, 0, nc.vector.tensor_copy)
+        quantise_x(0, 0, 1)
+        regroup(0, 1, nc.vector.tensor_copy)
+        quantise_w(0, 0, 1)
+        flip(0, 1)
+        flip(0, 2)
+        flip(0, 3)
+        quantise_w(0, 1, 1)
+        quantise_x(0, 1, 1)
+        project_group(0)
+        quantise_x(0, 2, 2)
+
+        S = nc.scalar.copy
+        before = {
+            1: [lambda: quantise_x(1, 0, 2)],
+            2: [lambda: quantise_x(1, 2, 2)],
+            3: [lambda: quantise_w(1, 0, 2)],
+            6: [lambda: quantise_w(4, 0, 2)],
+            7: [lambda: quantise_w(2, 0, 2)],
+            10: [lambda: quantise_w(5, 0, 2)],
+            11: [lambda: quantise_w(3, 0, 2)],
+        }
+        tensor_first = {
+            0: [lambda: flip(1, 0), lambda: flip(1, 1)],
+            1: [lambda: flip(1, 2), lambda: flip(1, 3)],
+        }
+        scalar_work = {
+            0: [lambda: regroup(1, 0, S)],
+            1: [lambda: regroup(1, 1, S)],
+            2: [lambda: regroup(4, 0, S), lambda: regroup(4, 1, S)],
+            3: [lambda: regroup(2, 0, S), lambda: regroup(2, 1, S)],
+            6: [lambda: plain_bank(0), lambda: plain_bank(1), lambda: plain_bank(2), lambda: plain_bank(3), lambda: regroup(5, 0, S)],
+            7: [lambda: plain_bank(4), lambda: plain_bank(5), lambda: plain_bank(6), lambda: plain_bank(7), lambda: regroup(5, 1, S)],
+            8: [lambda: regroup(3, 0, S), lambda: regroup(3, 1, S)],
+            10: [lambda: plain_bank(8), lambda: plain_bank(9), lambda: plain_bank(10), lambda: plain_bank(11)],
+            11: [lambda: plain_bank(12), lambda: plain_bank(13), lambda: plain_bank(14), lambda: plain_bank(15)],
+        }
+        for i in range(len(groups)):
+            for job in before.get(i, []):
+                job()
+            for job in tensor_first.get(i, []):
+                job()
+            if i + 1 < len(groups):
+                project_group(i + 1)
+            for job in scalar_work.get(i, []):
+                job()
+            rotate_group(i)

@@ -79,17 +79,13 @@ def build_rope_tables(nc, pool):
     cos_turns = pool.tile(shape, F32)
     wrap_turns(nc, pool, cos_turns[:], quarter_on[:], "nearest_cos")
 
-    cos_both = pool.tile([P, TOKEN_TILES, HD], F32)
+    factors = pool.tile([P, TOKEN_TILES, 2, PAIRS, 2], F32)
     nc.scalar.activation(
-        out=cos_both[:].rearrange("p j (i e) -> p j i e", e=2),
-        in_=cos_turns[:].unsqueeze(3).to_broadcast(shape + [2]),
-        func=ACT.Sin,
-        scale=TURN,
+        out=factors[:, :, 0], in_=cos_turns[:].unsqueeze(3).to_broadcast(shape + [2]), func=ACT.Sin, scale=TURN
     )
-    sin_signed = pool.tile([P, TOKEN_TILES, PAIRS, 2], F32)
-    nc.scalar.activation(out=sin_signed[:, :, :, 0], in_=sin_turns[:], func=ACT.Sin, scale=-TURN)
-    nc.scalar.activation(out=sin_signed[:, :, :, 1], in_=sin_turns[:], func=ACT.Sin, scale=TURN)
-    return cos_both, sin_signed
+    nc.scalar.activation(out=factors[:, :, 1, :, 0], in_=sin_turns[:], func=ACT.Sin, scale=TURN)
+    nc.scalar.activation(out=factors[:, :, 1, :, 1], in_=sin_turns[:], func=ACT.Sin, scale=-TURN)
+    return factors
 
 
 def tile_selfattention_pa_kernel(tc, x, w_qkv, out_0, out_1, out_2):
@@ -137,7 +133,7 @@ def tile_selfattention_pa_kernel(tc, x, w_qkv, out_0, out_1, out_2):
 
         identity = const.tile([P, P], F32)
         make_identity(nc, identity[:])
-        cos_both, sin_signed = build_rope_tables(nc, const)
+        factors = build_rope_tables(nc, const)
 
         w_grouped = {}
         w_codes = {}
@@ -219,28 +215,20 @@ def tile_selfattention_pa_kernel(tc, x, w_qkv, out_0, out_1, out_2):
                 if first_j == 0:
                     rope_result[(n, b)] = results.tile([P, CHUNK_HEADS, TOKEN_TILES, HD], F32, name="rotated")
                 rotated = rope_result[(n, b)][:, :, first_j : first_j + ADD_TILES, :]
-            by_cos = work.tile([P, CHUNK_HEADS, ADD_TILES, HD], F32, name="by_cos")
-            by_sin = work.tile([P, CHUNK_HEADS, ADD_TILES, HD], F32, name="by_sin")
+            products = work.tile([P, 2, CHUNK_HEADS, ADD_TILES, HD], F32, name="products")
+            both = [P, 2, CHUNK_HEADS, HD]
             for a in range(ADD_TILES):
-                j = first_j + a
-                bank = banks[i][a]
                 nc.vector.tensor_tensor(
-                    out=by_cos[:, :, a, :],
-                    in0=bank[:].rearrange("p (h d) -> p h d", h=CHUNK_HEADS),
-                    in1=cos_both[:, j, :].unsqueeze(1).to_broadcast([P, CHUNK_HEADS, HD]),
-                    op=ALU.mult,
-                )
-                nc.vector.tensor_tensor(
-                    out=by_sin[:, :, a, :].rearrange("p h (i e) -> p h i e", e=2),
-                    in0=bank[:].rearrange("p (h i e) -> p h i e", h=CHUNK_HEADS, e=2)[:, :, :, ::-1],
-                    in1=sin_signed[:, j].unsqueeze(1).to_broadcast([P, CHUNK_HEADS, PAIRS, 2]),
+                    out=products[:, :, :, a, :],
+                    in0=banks[i][a][:].rearrange("p (h d) -> p h d", h=CHUNK_HEADS).unsqueeze(1).to_broadcast(both),
+                    in1=factors[:, first_j + a].rearrange("p s i e -> p s (i e)").unsqueeze(2).to_broadcast(both),
                     op=ALU.mult,
                 )
             adder = nc.vector if i in VECTOR_ADDS else nc.gpsimd
             adder.tensor_tensor(
-                out=rotated.rearrange("p h a d -> p h (a d)"),
-                in0=by_cos[:].rearrange("p h a d -> p h (a d)"),
-                in1=by_sin[:].rearrange("p h a d -> p h (a d)"),
+                out=rotated.rearrange("p h a (i e) -> p h (a i) e", e=2),
+                in0=products[:, 0].rearrange("p h a (i e) -> p h (a i) e", e=2),
+                in1=products[:, 1].rearrange("p h a (i e) -> p h (a i) e", e=2)[:, :, :, ::-1],
                 op=ALU.add,
             )
             if last_unit:

@@ -126,10 +126,10 @@ def tile_selfattention_pa_kernel(tc, x, w_qkv, out_0, out_1, out_2):
         load_w(1, 1, 0)
         load_x(1, 2, 2)
         load_w(1, 1, 1)
-        load_w(4, 2, 0)
-        load_w(4, 2, 1)
         load_w(2, 2, 0)
         load_w(2, 2, 1)
+        load_w(4, 2, 0)
+        load_w(4, 2, 1)
 
         identity = const.tile([P, P], F32)
         make_identity(nc, identity[:])
@@ -266,10 +266,10 @@ def tile_selfattention_pa_kernel(tc, x, w_qkv, out_0, out_1, out_2):
             1: [lambda: quantise_x(1, 0, 2)],
             2: [lambda: quantise_x(1, 2, 2)],
             3: [lambda: quantise_w(1, 0, 2)],
-            6: [lambda: quantise_w(4, 0, 2)],
-            7: [lambda: quantise_w(2, 0, 2)],
-            10: [lambda: quantise_w(5, 0, 2)],
-            11: [lambda: quantise_w(3, 0, 2)],
+            6: [lambda: quantise_w(2, 0, 2)],
+            7: [lambda: quantise_w(4, 0, 2)],
+            10: [lambda: quantise_w(3, 0, 2)],
+            11: [lambda: quantise_w(5, 0, 2)],
         }
         tensor_first = {
             0: [lambda: flip(1, 0), lambda: flip(1, 1)],
@@ -278,13 +278,13 @@ def tile_selfattention_pa_kernel(tc, x, w_qkv, out_0, out_1, out_2):
         scalar_work = {
             0: [lambda: regroup(1, 0, S)],
             1: [lambda: regroup(1, 1, S)],
-            2: [lambda: regroup(4, 0, S), lambda: regroup(4, 1, S)],
-            3: [lambda: regroup(2, 0, S), lambda: regroup(2, 1, S)],
-            6: [lambda: plain_bank(0), lambda: plain_bank(1), lambda: plain_bank(2), lambda: plain_bank(3), lambda: regroup(5, 0, S)],
-            7: [lambda: plain_bank(4), lambda: plain_bank(5), lambda: plain_bank(6), lambda: plain_bank(7), lambda: regroup(5, 1, S)],
-            8: [lambda: regroup(3, 0, S), lambda: regroup(3, 1, S)],
-            10: [lambda: plain_bank(8), lambda: plain_bank(9), lambda: plain_bank(10), lambda: plain_bank(11)],
-            11: [lambda: plain_bank(12), lambda: plain_bank(13), lambda: plain_bank(14), lambda: plain_bank(15)],
+            2: [lambda: regroup(2, 0, S), lambda: regroup(2, 1, S)],
+            4: [lambda: regroup(4, 0, S), lambda: regroup(4, 1, S)],
+            6: [lambda: regroup(3, 0, S), lambda: regroup(3, 1, S)],
+            7: [lambda: regroup(5, 0, S), lambda: plain_bank(0), lambda: plain_bank(1), lambda: plain_bank(2), lambda: plain_bank(3)],
+            8: [lambda: regroup(5, 1, S), lambda: plain_bank(4), lambda: plain_bank(5), lambda: plain_bank(6), lambda: plain_bank(7)],
+            11: [lambda: plain_bank(8), lambda: plain_bank(9), lambda: plain_bank(10), lambda: plain_bank(11)],
+            12: [lambda: plain_bank(12), lambda: plain_bank(13), lambda: plain_bank(14), lambda: plain_bank(15)],
         }
         for i in range(len(groups)):
             for job in before.get(i, []):

@@ -117,8 +117,8 @@ def tile_selfattention_pa_kernel(tc, x, w_qkv, out_0, out_1, out_2):
         def load_x(b, j, tiles):
             nc.sync.dma_start(out=x_raw[:, b, j : j + tiles], in_=x_rows[b, :, j : j + tiles])
 
-        load_x(0, 0, 1)
         load_w(0, 1, 0)
+        load_x(0, 0, 1)
         load_w(0, 1, 1)
         load_x(0, 1, 1)
         load_x(0, 2, 2)
@@ -250,13 +250,15 @@ def tile_selfattention_pa_kernel(tc, x, w_qkv, out_0, out_1, out_2):
 
         flip(0, 0)
         regroup(0, 0, nc.vector.tensor_copy)
-        quantise_x(0, 0, 1)
-        regroup(0, 1, nc.vector.tensor_copy)
         quantise_w(0, 0, 1)
+        regroup(0, 1, nc.vector.tensor_copy)
+        quantise_w(0, 1, 1)
         flip(0, 1)
         flip(0, 2)
         flip(0, 3)
-        quantise_w(0, 1, 1)
+        flip(1, 0)
+        flip(1, 1)
+        quantise_x(0, 0, 1)
         quantise_x(0, 1, 1)
         project_group(0)
         quantise_x(0, 2, 2)
@@ -272,8 +274,7 @@ def tile_selfattention_pa_kernel(tc, x, w_qkv, out_0, out_1, out_2):
             11: [lambda: quantise_w(5, 0, 2)],
         }
         tensor_first = {
-            0: [lambda: flip(1, 0), lambda: flip(1, 1)],
-            1: [lambda: flip(1, 2), lambda: flip(1, 3)],
+            0: [lambda: flip(1, 2), lambda: flip(1, 3)],
         }
         scalar_work = {
             0: [lambda: regroup(1, 0, S)],

@@ -96,6 +96,7 @@ def tile_selfattention_pa_kernel(tc, x, w_qkv, out_0, out_1, out_2):
         grouped_pool = ctx.enter_context(tc.tile_pool(name="grouped", bufs=3))
         work = ctx.enter_context(tc.tile_pool(name="work", bufs=WORK_BUFS))
         results = ctx.enter_context(tc.tile_pool(name="results", bufs=3))
+        rotated_pool = ctx.enter_context(tc.tile_pool(name="rotated", bufs=6))
         psum = ctx.enter_context(tc.psum_pool(name="psum", bufs=4))
         ctx.enter_context(tc.manual_schedule())
 
@@ -199,7 +200,6 @@ def tile_selfattention_pa_kernel(tc, x, w_qkv, out_0, out_1, out_2):
 
         groups = [(n, b, j) for n in range(ROPE_CHUNKS) for b in range(B) for j in range(0, TOKEN_TILES, ADD_TILES)]
         banks = {}
-        rope_result = {}
 
         def project_group(i):
             n, b, first_j = groups[i]
@@ -207,14 +207,7 @@ def tile_selfattention_pa_kernel(tc, x, w_qkv, out_0, out_1, out_2):
 
         def rotate_group(i):
             n, b, first_j = groups[i]
-            last_unit = i >= len(groups) - TOKEN_TILES // ADD_TILES
-            if last_unit:
-                half = results.tile([P, CHUNK_HEADS, ADD_TILES, HD], F32, name="rotated")
-                rotated = half[:]
-            else:
-                if first_j == 0:
-                    rope_result[(n, b)] = results.tile([P, CHUNK_HEADS, TOKEN_TILES, HD], F32, name="rotated")
-                rotated = rope_result[(n, b)][:, :, first_j : first_j + ADD_TILES, :]
+            rotated = rotated_pool.tile([P, CHUNK_HEADS, ADD_TILES, HD], F32, name="rotated")
             products = work.tile([P, 2, CHUNK_HEADS, ADD_TILES, HD], F32, name="products")
             both = [P, 2, CHUNK_HEADS, HD]
             for a in range(ADD_TILES):
@@ -226,15 +219,12 @@ def tile_selfattention_pa_kernel(tc, x, w_qkv, out_0, out_1, out_2):
                 )
             adder = nc.vector if i in VECTOR_ADDS else nc.gpsimd
             adder.tensor_tensor(
-                out=rotated.rearrange("p h a (i e) -> p h (a i) e", e=2),
+                out=rotated[:].rearrange("p h a (i e) -> p h (a i) e", e=2),
                 in0=products[:, 0].rearrange("p h a (i e) -> p h (a i) e", e=2),
                 in1=products[:, 1].rearrange("p h a (i e) -> p h (a i) e", e=2)[:, :, :, ::-1],
                 op=ALU.add,
             )
-            if last_unit:
-                nc.sync.dma_start(out=destination(n, b)[:, :, first_j : first_j + ADD_TILES, :], in_=rotated)
-            elif first_j + ADD_TILES == TOKEN_TILES:
-                nc.sync.dma_start(out=destination(n, b), in_=rope_result[(n, b)][:])
+            nc.sync.dma_start(out=destination(n, b)[:, :, first_j : first_j + ADD_TILES, :], in_=rotated[:])
 
         plain = [(n, b, j) for n in range(ROPE_CHUNKS, ROPE_CHUNKS + PLAIN_CHUNKS) for b in range(B) for j in range(TOKEN_TILES)]
         plain_result = {}

@@ -207,7 +207,6 @@ def tile_selfattention_pa_kernel(tc, x, w_qkv, out_0, out_1, out_2):
 
         def rotate_group(i):
             n, b, first_j = groups[i]
-            rotated = rotated_pool.tile([P, CHUNK_HEADS, ADD_TILES, HD], F32, name="rotated")
             products = work.tile([P, 2, CHUNK_HEADS, ADD_TILES, HD], F32, name="products")
             both = [P, 2, CHUNK_HEADS, HD]
             for a in range(ADD_TILES):
@@ -217,8 +216,19 @@ def tile_selfattention_pa_kernel(tc, x, w_qkv, out_0, out_1, out_2):
                     in1=factors[:, first_j + a].rearrange("p s i e -> p s (i e)").unsqueeze(2).to_broadcast(both),
                     op=ALU.mult,
                 )
-            adder = nc.vector if i in VECTOR_ADDS else nc.gpsimd
-            adder.tensor_tensor(
+            if i in VECTOR_ADDS:
+                for a in range(ADD_TILES):
+                    last = rotated_pool.tile([P, CHUNK_HEADS, HD], F32, name="rotated")
+                    nc.vector.tensor_tensor(
+                        out=last[:].rearrange("p h (i e) -> p h i e", e=2),
+                        in0=products[:, 0, :, a, :].rearrange("p h (i e) -> p h i e", e=2),
+                        in1=products[:, 1, :, a, :].rearrange("p h (i e) -> p h i e", e=2)[:, :, :, ::-1],
+                        op=ALU.add,
+                    )
+                    nc.scalar.dma_start(out=destination(n, b)[:, :, first_j + a, :], in_=last[:])
+                return
+            rotated = rotated_pool.tile([P, CHUNK_HEADS, ADD_TILES, HD], F32, name="rotated")
+            nc.gpsimd.tensor_tensor(
                 out=rotated[:].rearrange("p h a (i e) -> p h (a i) e", e=2),
                 in0=products[:, 0].rearrange("p h a (i e) -> p h (a i) e", e=2),
                 in1=products[:, 1].rearrange("p h a (i e) -> p h (a i) e", e=2)[:, :, :, ::-1],

@@ -30,7 +30,7 @@ PLAIN_CHUNKS = E // CHUNK
 PAIRS = HD // 2
 DOUBLINGS = 6
 assert 2**DOUBLINGS == PAIRS
-RUN = 4
+RUN = 8
 ADD_TILES = 2
 WORK_BUFS = 4
 VECTOR_ADDS = (15,)

@@ -6,7 +6,6 @@ from concourse.masks import make_identity
 
 F32 = mybir.dt.float32
 BF16 = mybir.dt.bfloat16
-I32 = mybir.dt.int32
 U32 = mybir.dt.uint32
 U8 = mybir.dt.uint8
 FP8X4 = mybir.dt.float8_e4m3fn_x4
@@ -50,41 +49,43 @@ def wrap_turns(nc, pool, out, turns, name):
 
 def build_rope_tables(nc, pool):
     shape = [P, TOKEN_TILES, PAIRS]
-    token_int = pool.tile([P, TOKEN_TILES], I32)
-    nc.gpsimd.iota(token_int[:], pattern=[[1, TOKEN_TILES]], base=0, channel_multiplier=TOKEN_TILES)
     token = pool.tile([P, TOKEN_TILES], F32)
-    nc.vector.tensor_copy(out=token[:], in_=token_int[:])
+    nc.gpsimd.iota(
+        token[:], pattern=[[1, TOKEN_TILES]], base=0, channel_multiplier=TOKEN_TILES, allow_small_or_imprecise_dtypes=True
+    )
 
-    one = pool.tile([P, 1], F32)
-    nc.vector.memset(one[:], 1.0)
-    turns_per_token = pool.tile([P, PAIRS], F32)
-    nc.vector.tensor_scalar_mul(out=turns_per_token[:, 0:1], in0=one[:], scalar1=1.0 / TURN)
+    ratios = pool.tile([P, PAIRS], F32)
+    nc.vector.memset(ratios[:, 0:1], 1.0)
     for doubling in range(DOUBLINGS):
         width = 2**doubling
-        nc.vector.tensor_scalar_mul(
-            out=turns_per_token[:, width : 2 * width], in0=turns_per_token[:, 0:width], scalar1=FREQ_RATIO**width
-        )
+        nc.vector.tensor_scalar_mul(out=ratios[:, width : 2 * width], in0=ratios[:, 0:width], scalar1=FREQ_RATIO**width)
 
     turns = pool.tile(shape, F32)
-    nc.vector.tensor_tensor(
+    nc.vector.scalar_tensor_tensor(
         out=turns[:],
         in0=token[:].unsqueeze(2).to_broadcast(shape),
-        in1=turns_per_token[:].unsqueeze(1).to_broadcast(shape),
-        op=ALU.mult,
+        scalar=1.0 / TURN,
+        in1=ratios[:].unsqueeze(1).to_broadcast(shape),
+        op0=ALU.mult,
+        op1=ALU.mult,
     )
     sin_turns = pool.tile(shape, F32)
     wrap_turns(nc, pool, sin_turns[:], turns[:], "nearest_sin")
-    quarter_on = pool.tile(shape, F32)
-    nc.vector.tensor_scalar_add(out=quarter_on[:], in0=sin_turns[:], scalar1=0.25)
-    cos_turns = pool.tile(shape, F32)
-    wrap_turns(nc, pool, cos_turns[:], quarter_on[:], "nearest_cos")
+    size_turns = pool.tile(shape, F32)
+    nc.vector.scalar_tensor_tensor(
+        out=size_turns[:], in0=sin_turns[:], scalar=-1.0, in1=sin_turns[:], op0=ALU.mult, op1=ALU.max
+    )
 
     factors = pool.tile([P, TOKEN_TILES, 2, PAIRS, 2], F32)
-    nc.scalar.activation(
-        out=factors[:, :, 0], in_=cos_turns[:].unsqueeze(3).to_broadcast(shape + [2]), func=ACT.Sin, scale=TURN
-    )
     nc.scalar.activation(out=factors[:, :, 1, :, 0], in_=sin_turns[:], func=ACT.Sin, scale=TURN)
     nc.scalar.activation(out=factors[:, :, 1, :, 1], in_=sin_turns[:], func=ACT.Sin, scale=-TURN)
+    nc.scalar.activation(
+        out=factors[:, :, 0],
+        in_=size_turns[:].unsqueeze(3).to_broadcast(shape + [2]),
+        func=ACT.Sin,
+        scale=-TURN,
+        bias=TURN / 4.0,
+    )
     return factors
 
 
@@ -132,9 +133,9 @@ def tile_selfattention_pa_kernel(tc, x, w_qkv, out_0, out_1, out_2):
         load_w(4, 2, 0)
         load_w(4, 2, 1)
 
+        factors = build_rope_tables(nc, const)
         identity = const.tile([P, P], F32)
         make_identity(nc, identity[:])
-        factors = build_rope_tables(nc, const)
 
         w_grouped = {}
         w_codes = {}

@@ -271,8 +271,7 @@ def tile_selfattention_pa_kernel(tc, x, w_qkv, out_0, out_1, out_2):
             3: [lambda: quantise_w(1, 0, 2)],
             6: [lambda: quantise_w(2, 0, 2)],
             7: [lambda: quantise_w(4, 0, 2)],
-            10: [lambda: quantise_w(3, 0, 2)],
-            11: [lambda: quantise_w(5, 0, 2)],
+            10: [lambda: quantise_w(3, 0, 2), lambda: quantise_w(5, 0, 2)],
         }
         tensor_first = {
             0: [lambda: flip(1, 2), lambda: flip(1, 3)],
@@ -285,8 +284,8 @@ def tile_selfattention_pa_kernel(tc, x, w_qkv, out_0, out_1, out_2):
             6: [lambda: regroup(3, 0, S), lambda: regroup(3, 1, S)],
             7: [lambda: regroup(5, 0, S), lambda: plain_bank(0), lambda: plain_bank(1), lambda: plain_bank(2), lambda: plain_bank(3)],
             8: [lambda: regroup(5, 1, S), lambda: plain_bank(4), lambda: plain_bank(5), lambda: plain_bank(6), lambda: plain_bank(7)],
-            11: [lambda: plain_bank(8), lambda: plain_bank(9), lambda: plain_bank(10), lambda: plain_bank(11)],
-            12: [lambda: plain_bank(12), lambda: plain_bank(13), lambda: plain_bank(14), lambda: plain_bank(15)],
+            10: [lambda: plain_bank(8), lambda: plain_bank(9), lambda: plain_bank(10), lambda: plain_bank(11)],
+            11: [lambda: plain_bank(12), lambda: plain_bank(13), lambda: plain_bank(14), lambda: plain_bank(15)],
         }
         for i in range(len(groups)):
             for job in before.get(i, []):

@@ -134,8 +134,16 @@ def tile_selfattention_pa_kernel(tc, x, w_qkv, out_0, out_1, out_2):
         load_w(4, 2, 1)
 
         factors = build_rope_tables(nc, const)
+        idle_operand = const.tile([P, CHUNK], BF16)
+        nc.gpsimd.memset(idle_operand[:], 0.0)
         identity = const.tile([P, P], F32)
         make_identity(nc, identity[:])
+
+        idle_bank = psum.tile([P, CHUNK], F32, name="idle_bank", tag="rope")
+
+        def keep_warm(times):
+            for unused in range(times):
+                nc.tensor.matmul(idle_bank[:], lhsT=idle_operand[:, 0:P], rhs=idle_operand[:], start=True, stop=True)
 
         w_grouped = {}
         w_codes = {}
@@ -249,12 +257,15 @@ def tile_selfattention_pa_kernel(tc, x, w_qkv, out_0, out_1, out_2):
             if j == TOKEN_TILES - 1:
                 nc.scalar.dma_start(out=destination(n, b), in_=plain_result[(n, b)][:])
 
+        keep_warm(9)
         flip(0, 0)
+        keep_warm(2)
         regroup(0, 0, nc.vector.tensor_copy)
         quantise_w(0, 0, 1)
         regroup(0, 1, nc.vector.tensor_copy)
         quantise_w(0, 1, 1)
         flip(0, 1)
+        keep_warm(1)
         flip(0, 2)
         flip(0, 3)
         flip(1, 0)

import math
from contextlib import ExitStack

import concourse.mybir as mybir
from concourse.masks import make_identity

F32 = mybir.dt.float32
BF16 = mybir.dt.bfloat16
U32 = mybir.dt.uint32
U8 = mybir.dt.uint8
FP8X4 = mybir.dt.float8_e4m3fn_x4
ALU = mybir.AluOpType
ACT = mybir.ActivationFunctionType

B, T, D, H, HD = 2, 512, 1024, 8, 128
E = H * HD
FLOPS = 2 * B * T * D * 3 * E

P = 128
PACK = 4
K_PASS = P * PACK
PASSES = D // K_PASS
WORDS = PACK // 2
TOKEN_TILES = T // P
CHUNK = 512
CHUNK_HEADS = CHUNK // HD
ROPE_CHUNKS = 2 * E // CHUNK
PLAIN_CHUNKS = E // CHUNK
PAIRS = HD // 2
DOUBLINGS = 6
assert 2**DOUBLINGS == PAIRS
RUN = 8
ADD_TILES = 2
WORK_BUFS = 4
VECTOR_ADDS = (15,)

TURN = 2.0 * math.pi
FREQ_RATIO = 10000.0 ** (-2.0 / HD)
ROUND_MAGIC = 1.5 * 2.0**23


def wrap_turns(nc, pool, out, turns, name):
    nearest = pool.tile([P, TOKEN_TILES, PAIRS], F32, name=name)
    nc.vector.tensor_scalar(
        out=nearest[:], in0=turns, scalar1=ROUND_MAGIC, scalar2=ROUND_MAGIC, op0=ALU.add, op1=ALU.subtract
    )
    nc.vector.tensor_tensor(out=out, in0=turns, in1=nearest[:], op=ALU.subtract)


def build_rope_tables(nc, pool):
    shape = [P, TOKEN_TILES, PAIRS]
    token = pool.tile([P, TOKEN_TILES], F32)
    nc.gpsimd.iota(
        token[:], pattern=[[1, TOKEN_TILES]], base=0, channel_multiplier=TOKEN_TILES, allow_small_or_imprecise_dtypes=True
    )

    ratios = pool.tile([P, PAIRS], F32)
    nc.vector.memset(ratios[:, 0:1], 1.0)
    for doubling in range(DOUBLINGS):
        width = 2**doubling
        nc.vector.tensor_scalar_mul(out=ratios[:, width : 2 * width], in0=ratios[:, 0:width], scalar1=FREQ_RATIO**width)

    turns = pool.tile(shape, F32)
    nc.vector.scalar_tensor_tensor(
        out=turns[:],
        in0=token[:].unsqueeze(2).to_broadcast(shape),
        scalar=1.0 / TURN,
        in1=ratios[:].unsqueeze(1).to_broadcast(shape),
        op0=ALU.mult,
        op1=ALU.mult,
    )
    sin_turns = pool.tile(shape, F32)
    wrap_turns(nc, pool, sin_turns[:], turns[:], "nearest_sin")
    size_turns = pool.tile(shape, F32)
    nc.vector.scalar_tensor_tensor(
        out=size_turns[:], in0=sin_turns[:], scalar=-1.0, in1=sin_turns[:], op0=ALU.mult, op1=ALU.max
    )

    factors = pool.tile([P, TOKEN_TILES, 2, PAIRS, 2], F32)
    nc.scalar.activation(out=factors[:, :, 1, :, 0], in_=sin_turns[:], func=ACT.Sin, scale=TURN)
    nc.scalar.activation(out=factors[:, :, 1, :, 1], in_=sin_turns[:], func=ACT.Sin, scale=-TURN)
    nc.scalar.activation(
        out=factors[:, :, 0],
        in_=size_turns[:].unsqueeze(3).to_broadcast(shape + [2]),
        func=ACT.Sin,
        scale=-TURN,
        bias=TURN / 4.0,
    )
    return factors


def tile_selfattention_pa_kernel(tc, x, w_qkv, out_0, out_1, out_2):
    nc = tc.nc
    with ExitStack() as ctx:
        const = ctx.enter_context(tc.tile_pool(name="const", bufs=1))
        keep = ctx.enter_context(tc.tile_pool(name="keep", bufs=1))
        grouped_pool = ctx.enter_context(tc.tile_pool(name="grouped", bufs=3))
        work = ctx.enter_context(tc.tile_pool(name="work", bufs=WORK_BUFS))
        results = ctx.enter_context(tc.tile_pool(name="results", bufs=3))
        rotated_pool = ctx.enter_context(tc.tile_pool(name="rotated", bufs=6))
        psum = ctx.enter_context(tc.psum_pool(name="psum", bufs=4))
        ctx.enter_context(tc.manual_schedule())

        warm = const.tile([P, 1], F32)
        nc.vector.memset(warm[:], 0.0)
        nc.scalar.activation(out=warm[:], in_=warm[:], func=ACT.Sin)

        x_raw = keep.tile([P, B, TOKEN_TILES, D], BF16)
        x_rows = x.rearrange("b (p j) k -> b p j k", j=TOKEN_TILES)
        w_rows = w_qkv.rearrange("(g p r) c -> g p r c", g=PASSES, r=PACK)
        w_raw = {}

        def load_w(first_chunk, chunks, g):
            piece = keep.tile([P, PACK, chunks * CHUNK], BF16, name="w_raw%d_%d" % (first_chunk, g))
            nc.sync.dma_start(out=piece[:], in_=w_rows[g, :, :, first_chunk * CHUNK : (first_chunk + chunks) * CHUNK])
            for c in range(chunks):
                w_raw[(first_chunk + c, g)] = piece[:, :, c * CHUNK : (c + 1) * CHUNK]

        def load_x(b, j, tiles):
            nc.sync.dma_start(out=x_raw[:, b, j : j + tiles], in_=x_rows[b, :, j : j + tiles])

        load_w(0, 1, 0)
        load_x(0, 0, 1)
        load_w(0, 1, 1)
        load_x(0, 1, 1)
        load_x(0, 2, 2)
        load_x(1, 0, 2)
        load_w(1, 1, 0)
        load_x(1, 2, 2)
        load_w(1, 1, 1)
        load_w(2, 2, 0)
        load_w(2, 2, 1)
        load_w(4, 2, 0)
        load_w(4, 2, 1)

        factors = build_rope_tables(nc, const)
        idle_operand = const.tile([P, CHUNK], BF16)
        nc.gpsimd.memset(idle_operand[:], 0.0)
        identity = const.tile([P, P], F32)
        make_identity(nc, identity[:])

        idle_bank = psum.tile([P, CHUNK], F32, name="idle_bank", tag="rope")

        def keep_warm(times):
            for unused in range(times):
                nc.tensor.matmul(idle_bank[:], lhsT=idle_operand[:, 0:P], rhs=idle_operand[:], start=True, stop=True)

        w_grouped = {}
        w_codes = {}
        w_scales = {}

        def regroup(n, g, copy):
            if n not in w_grouped:
                w_grouped[n] = grouped_pool.tile([P, PASSES, CHUNK, PACK], BF16, name="w_grouped", align_bytes=64)
            copy(
                out=w_grouped[n][:, g].rearrange("p (c i) r -> p c r i", i=RUN),
                in_=w_raw[(n, g)].rearrange("p r (c i) -> p c r i", i=RUN),
            )

        def quantise_w(n, first_g, passes):
            if n not in w_codes:
                w_codes[n] = keep.tile([P, PASSES, CHUNK], U32, name="w_codes%d" % n, align_bytes=64)
                w_scales[n] = keep.tile([P, PASSES, CHUNK], U8, name="w_scales%d" % n, align_bytes=64)
            gs = slice(first_g, first_g + passes)
            nc.vector.quantize_mx(
                out=w_codes[n][:, gs].rearrange("p g c -> p (g c)").bitcast(FP8X4),
                scales=w_scales[n][:, gs].rearrange("p g c -> p (g c)"),
                in_=w_grouped[n][:, gs].rearrange("p g c r -> p (g c r)"),
            )

        x_grouped = keep.tile([P, B, TOKEN_TILES, PASSES, P, PACK], BF16, align_bytes=64)
        x_codes = keep.tile([P, B, TOKEN_TILES, PASSES, P], U32, align_bytes=64)
        x_scales = keep.tile([P, B, TOKEN_TILES, PASSES, P], U8, align_bytes=64)
        x_words = x_raw[:].bitcast(F32).rearrange("p b j (g q u) -> p b j g u q", g=PASSES, u=WORDS)

        def flip(b, j):
            flipped = psum.tile([P, PASSES, WORDS, P], F32, name="flipped", tag="plain")
            for g in range(PASSES):
                for u in range(WORDS):
                    nc.tensor.transpose(flipped[:, g, u, :], x_words[:, b, j, g, u, :], identity[:])
            nc.scalar.copy(out=x_grouped[:, b, j].bitcast(F32), in_=flipped[:].rearrange("p g u t -> p g t u"))

        def quantise_x(b, j, tiles):
            js = slice(j, j + tiles)
            nc.vector.quantize_mx(
                out=x_codes[:, b, js].rearrange("p j g t -> p (j g t)").bitcast(FP8X4),
                scales=x_scales[:, b, js].rearrange("p j g t -> p (j g t)"),
                in_=x_grouped[:, b, js].rearrange("p j g t r -> p (j g t r)"),
            )

        def project(n, b, j, tag):
            bank = psum.tile([P, CHUNK], F32, name="bank_" + tag, tag=tag)
            for g in range(PASSES):
                nc.tensor.matmul_mx(
                    out=bank[:],
                    lhsT=x_codes[:, b, j, g, :].bitcast(FP8X4),
                    lhsT_scale=x_scales[:, b, j, g, :],
                    rhs=w_codes[n][:, g, :].bitcast(FP8X4),
                    rhs_scale=w_scales[n][:, g, :],
                    start=(g == 0),
                    stop=(g == PASSES - 1),
                )
            return bank

        def destination(n, b):
            out = (out_0, out_1, out_2)[n * CHUNK // E]
            first_head = n * CHUNK % E // HD
            return out[b, first_head : first_head + CHUNK_HEADS].rearrange("h (p j) d -> p h j d", j=TOKEN_TILES)

        groups = [(n, b, j) for n in range(ROPE_CHUNKS) for b in range(B) for j in range(0, TOKEN_TILES, ADD_TILES)]
        banks = {}

        def project_group(i):
            n, b, first_j = groups[i]
            banks[i] = [project(n, b, first_j + a, "rope") for a in range(ADD_TILES)]

        def rotate_group(i):
            n, b, first_j = groups[i]
            products = work.tile([P, 2, CHUNK_HEADS, ADD_TILES, HD], F32, name="products")
            both = [P, 2, CHUNK_HEADS, HD]
            for a in range(ADD_TILES):
                nc.vector.tensor_tensor(
                    out=products[:, :, :, a, :],
                    in0=banks[i][a][:].rearrange("p (h d) -> p h d", h=CHUNK_HEADS).unsqueeze(1).to_broadcast(both),
                    in1=factors[:, first_j + a].rearrange("p s i e -> p s (i e)").unsqueeze(2).to_broadcast(both),
                    op=ALU.mult,
                )
            if i in VECTOR_ADDS:
                for a in range(ADD_TILES):
                    last = rotated_pool.tile([P, CHUNK_HEADS, HD], F32, name="rotated")
                    nc.vector.tensor_tensor(
                        out=last[:].rearrange("p h (i e) -> p h i e", e=2),
                        in0=products[:, 0, :, a, :].rearrange("p h (i e) -> p h i e", e=2),
                        in1=products[:, 1, :, a, :].rearrange("p h (i e) -> p h i e", e=2)[:, :, :, ::-1],
                        op=ALU.add,
                    )
                    nc.scalar.dma_start(out=destination(n, b)[:, :, first_j + a, :], in_=last[:])
                return
            rotated = rotated_pool.tile([P, CHUNK_HEADS, ADD_TILES, HD], F32, name="rotated")
            nc.gpsimd.tensor_tensor(
                out=rotated[:].rearrange("p h a (i e) -> p h (a i) e", e=2),
                in0=products[:, 0].rearrange("p h a (i e) -> p h (a i) e", e=2),
                in1=products[:, 1].rearrange("p h a (i e) -> p h (a i) e", e=2)[:, :, :, ::-1],
                op=ALU.add,
            )
            nc.sync.dma_start(out=destination(n, b)[:, :, first_j : first_j + ADD_TILES, :], in_=rotated[:])

        plain = [(n, b, j) for n in range(ROPE_CHUNKS, ROPE_CHUNKS + PLAIN_CHUNKS) for b in range(B) for j in range(TOKEN_TILES)]
        plain_result = {}

        def plain_bank(k):
            n, b, j = plain[k]
            if j == 0:
                plain_result[(n, b)] = results.tile([P, CHUNK_HEADS, TOKEN_TILES, HD], F32, name="copied")
            bank = project(n, b, j, "plain")
            nc.scalar.copy(out=plain_result[(n, b)][:, :, j, :], in_=bank[:].rearrange("p (h d) -> p h d", h=CHUNK_HEADS))
            if j == TOKEN_TILES - 1:
                nc.scalar.dma_start(out=destination(n, b), in_=plain_result[(n, b)][:])

        keep_warm(9)
        flip(0, 0)
        keep_warm(2)
        regroup(0, 0, nc.vector.tensor_copy)
        quantise_w(0, 0, 1)
        regroup(0, 1, nc.vector.tensor_copy)
        quantise_w(0, 1, 1)
        flip(0, 1)
        keep_warm(1)
        flip(0, 2)
        flip(0, 3)
        flip(1, 0)
        flip(1, 1)
        quantise_x(0, 0, 1)
        quantise_x(0, 1, 1)
        project_group(0)
        quantise_x(0, 2, 2)

        S = nc.scalar.copy
        before = {
            1: [lambda: quantise_x(1, 0, 2)],
            2: [lambda: quantise_x(1, 2, 2)],
            3: [lambda: quantise_w(1, 0, 2)],
            6: [lambda: quantise_w(2, 0, 2)],
            7: [lambda: quantise_w(4, 0, 2)],
            10: [lambda: quantise_w(3, 0, 2), lambda: quantise_w(5, 0, 2)],
        }
        tensor_first = {
            0: [lambda: flip(1, 2), lambda: flip(1, 3)],
        }
        scalar_work = {
            0: [lambda: regroup(1, 0, S)],
            1: [lambda: regroup(1, 1, S)],
            2: [lambda: regroup(2, 0, S), lambda: regroup(2, 1, S)],
            4: [lambda: regroup(4, 0, S), lambda: regroup(4, 1, S)],
            6: [lambda: regroup(3, 0, S), lambda: regroup(3, 1, S)],
            7: [lambda: regroup(5, 0, S), lambda: plain_bank(0), lambda: plain_bank(1), lambda: plain_bank(2), lambda: plain_bank(3)],
            8: [lambda: regroup(5, 1, S), lambda: plain_bank(4), lambda: plain_bank(5), lambda: plain_bank(6), lambda: plain_bank(7)],
            10: [lambda: plain_bank(8), lambda: plain_bank(9), lambda: plain_bank(10), lambda: plain_bank(11)],
            11: [lambda: plain_bank(12), lambda: plain_bank(13), lambda: plain_bank(14), lambda: plain_bank(15)],
        }
        for i in range(len(groups)):
            for job in before.get(i, []):
                job()
            for job in tensor_first.get(i, []):
                job()
            if i + 1 < len(groups):
                project_group(i + 1)
            for job in scalar_work.get(i, []):
                job()
            rotate_group(i)
